import numpy as np
import ml_dtypes


def mxq(x, axis, fmt="e4m3"):
    dtype, down = {"e4m3": (ml_dtypes.float8_e4m3fn, 7), "e5m2": (ml_dtypes.float8_e5m2, 14)}[fmt]
    v = np.moveaxis(np.asarray(x, np.float32).astype(ml_dtypes.bfloat16).astype(np.float64), axis, -1)
    blocks = v.reshape(v.shape[:-1] + (-1, 32))
    amax = np.abs(blocks).max(-1, keepdims=True)
    byte = np.maximum(np.where(amax > 0, np.frexp(amax)[1] - 1 + 127, 0) - down, 1)
    scale = np.exp2(byte - 127.0)
    codes = (blocks / scale).astype(np.float32).astype(dtype).astype(np.float64)
    return np.moveaxis((codes * scale).reshape(v.shape), -1, axis)


WIDE = False


def mx_kscale(k):
    if not WIDE:
        return np.ones(k)
    levels = np.array([10, -10, 5, -5, 0])
    a = np.random.permutation(np.resize(levels, k // 512 * 4)).reshape(k // 512, 4)
    idx = np.arange(k)
    return np.exp2(a[idx // 512, idx % 128 // 32])


BF16 = ml_dtypes.bfloat16


def bf(x):
    return np.asarray(x, np.float32).astype(BF16)


def f64(x):
    return np.asarray(x).astype(np.float64)


B, S, D, QK, EXP = 2, 512, 1024, 128, 2048
EPS = 1e-5
W = QK + QK + EXP + EXP
NT = 110


def erf(v):
    a = np.minimum(np.abs(v), 6.0)
    c = 2.0 * a * a
    term = a.copy()
    total = a.copy()
    for n in range(1, NT):
        term = term * c / (2.0 * n + 1.0)
        total = total + term
    return np.sign(v) * (2.0 / np.sqrt(np.pi)) * np.exp(-a * a) * total


def gelu(v):
    return 0.5 * v * (1.0 + erf(v / np.sqrt(2.0)))


def setup_inputs():
    s = mx_kscale(D)
    row_gain = np.exp(0.5 * np.random.standard_normal((B, S)))[..., None]
    row_shift = 0.5 * np.random.standard_normal((B, S))[..., None]
    return {"x": bf(np.random.standard_normal((B, S, D)) * row_gain + row_shift),
            "ln_gamma": bf((1.0 + 0.1 * np.random.standard_normal(D)) * s),
            "ln_beta": bf(0.1 * np.random.standard_normal(D) * s),
            "expand": bf(np.random.standard_normal((W, D)) / np.sqrt(D) / s[None, :])}


def reference(x, ln_gamma, ln_beta, expand):
    x = f64(x)
    mu = x.mean(-1, keepdims=True)
    var = x.var(-1, keepdims=True)
    h = (x - mu) / np.sqrt(var + EPS) * f64(ln_gamma) + f64(ln_beta)
    fused = mxq(h, 2, "e4m3") @ mxq(f64(expand), 1, "e4m3").T
    query = fused[..., :QK]
    key = fused[..., QK:QK + QK]
    linear = fused[..., QK + QK:QK + QK + EXP]
    pre_gelu = fused[..., QK + QK + EXP:]
    geglu = linear * gelu(pre_gelu)
    return query, key, geglu

@@ -1,0 +1,278 @@
+from contextlib import ExitStack
+
+import concourse.mybir as mybir
+from concourse.masks import make_identity
+
+F32 = mybir.dt.float32
+BF16 = mybir.dt.bfloat16
+U32 = mybir.dt.uint32
+U8 = mybir.dt.uint8
+FP8X4 = mybir.dt.float8_e4m3fn_x4
+ACT = mybir.ActivationFunctionType
+ALU = mybir.AluOpType
+
+P = 128
+TOKENS = 1024
+D = 1024
+QK = 128
+EXP = 2048
+EPS = 1e-5
+
+PACK = 4
+PASSES = D // (P * PACK)
+BANK = 512
+CHUNK = 512
+ROUNDS = EXP // CHUNK
+GROUP_TILES = 2
+GROUP = GROUP_TILES * P
+GROUPS = TOKENS // GROUP
+FEATURE_TILES = D // P
+LOOKAHEAD = 4
+
+FLOPS = 2 * TOKENS * D * (2 * QK + 2 * EXP)
+
+
+def tile_latentattentionblock_pa_kernel(tc, x, ln_gamma, ln_beta, expand, out_0, out_1, out_2):
+    nc = tc.nc
+    x_rows = x.flatten_outer_dims()
+    query = out_0.flatten_outer_dims()
+    key = out_1.flatten_outer_dims()
+    geglu = out_2.flatten_outer_dims()
+
+    chunks = []
+    for j in range(ROUNDS):
+        chunks.append((2 * QK + EXP + j * CHUNK, CHUNK))
+        chunks.append((2 * QK + j * CHUNK, CHUNK))
+    QK_CHUNK = len(chunks)
+    chunks.append((0, 2 * QK))
+
+    preparations = [("rows", 0), ("tokens", 0), ("rows", 1), ("tokens", 1)]
+    preparations.extend([("rows", c) for c in range(2, QK_CHUNK)])
+    preparations.extend([("tokens", 2), ("tokens", 3), ("rows", QK_CHUNK)])
+
+    with ExitStack() as ctx:
+        keep = ctx.enter_context(tc.tile_pool(name="keep", bufs=1))
+        small = ctx.enter_context(tc.tile_pool(name="small", bufs=4))
+        normed = ctx.enter_context(tc.tile_pool(name="normed", bufs=2 * GROUP_TILES))
+        stage = ctx.enter_context(tc.tile_pool(name="stage", bufs=2))
+        rows_stage = ctx.enter_context(tc.tile_pool(name="rows_stage", bufs=3))
+        result = ctx.enter_context(tc.tile_pool(name="result", bufs=4))
+        psum = ctx.enter_context(tc.psum_pool(name="psum", bufs=8))
+        ctx.enter_context(tc.manual_schedule())
+
+        gain_rows = keep.tile([P, 2 * P], BF16, name="gain_rows")
+        nc.gpsimd.memset(gain_rows[:], 0.0)
+        ident = keep.tile([P, P], F32, name="ident")
+        make_identity(nc, ident[:])
+        minus_half = keep.tile([P, 1], F32, name="minus_half")
+        nc.gpsimd.memset(minus_half[:], -0.5)
+
+        x_sb = [keep.tile([P, GROUP_TILES * D], BF16, name="x_sb%d" % g) for g in range(GROUPS)]
+        e_sb = [keep.tile([P, (rows // P) * D], BF16, name="e_sb%d" % c) for c, (first, rows) in enumerate(chunks)]
+
+        def load_tokens(g):
+            nc.sync.dma_start(
+                out=x_sb[g][:].rearrange("p (t k) -> p t k", k=D),
+                in_=x_rows[g * GROUP : (g + 1) * GROUP, :].rearrange("(t p) k -> p t k", p=P),
+            )
+
+        def load_rows(c):
+            first, rows = chunks[c]
+            nc.sync.dma_start(
+                out=e_sb[c][:].rearrange("p (t k) -> p t k", k=D),
+                in_=expand[first : first + rows, :].rearrange("(t p) k -> p t k", p=P),
+            )
+
+        load_tokens(0)
+        nc.sync.dma_start(out=gain_rows[0:4, :], in_=ln_gamma.rearrange("(r c) -> r c", r=4))
+        nc.sync.dma_start(out=gain_rows[4:8, :], in_=ln_beta.rearrange("(r c) -> r c", r=4))
+        load_tokens(1)
+        for c in range(4):
+            load_rows(c)
+        load_tokens(2)
+        load_tokens(3)
+        for c in range(4, len(chunks)):
+            load_rows(c)
+
+        h_words = [keep.tile([P, PASSES * GROUP], U32, name="h_words%d" % g, align_bytes=64) for g in range(GROUPS)]
+        h_scales = [keep.tile([P, PASSES * GROUP], U8, name="h_scales%d" % g, align_bytes=64) for g in range(GROUPS)]
+        e_words = [
+            keep.tile([P, PASSES * rows], U32, name="e_words%d" % c, align_bytes=64) for c, (first, rows) in enumerate(chunks)
+        ]
+        e_scales = [
+            keep.tile([P, PASSES * rows], U8, name="e_scales%d" % c, align_bytes=64) for c, (first, rows) in enumerate(chunks)
+        ]
+
+        xn = {}
+        banks_of = {}
+        staged = {}
+
+        def normalise(i):
+            g, t = divmod(i, GROUP_TILES)
+            x_tile = x_sb[g][:, t * D : (t + 1) * D]
+            stats = small.tile([P, 2, 6], F32, tag="stats")
+            for s in range(2):
+                nc.vector.bn_stats(out=stats[:, s, :], in_=x_tile[:, s * 512 : (s + 1) * 512])
+            mean_var = small.tile([P, 2], F32, tag="mean_var")
+            nc.vector.bn_aggr(out=mean_var[:], in_=stats[:].rearrange("p s c -> p (s c)"))
+            var_eps = small.tile([P, 1], F32, tag="var_eps")
+            nc.gpsimd.tensor_scalar(
+                out=var_eps[:], in0=mean_var[:, 1:2], scalar1=EPS, scalar2=1.0, op0=ALU.add, op1=ALU.mult
+            )
+            rstd = small.tile([P, 1], F32, tag="rstd")
+            nc.gpsimd.tensor_tensor(out=rstd[:], in0=var_eps[:], in1=minus_half[:], op=ALU.pow)
+            minus_mean = small.tile([P, 1], F32, tag="minus_mean")
+            nc.gpsimd.tensor_scalar(
+                out=minus_mean[:], in0=mean_var[:, 0:1], scalar1=-1.0, scalar2=0.0, op0=ALU.mult, op1=ALU.add
+            )
+            xn[i] = normed.tile([P, FEATURE_TILES, P], F32, tag="xn", name="xn")
+            nc.gpsimd.tensor_scalar(
+                out=xn[i][:].rearrange("p (c e) q -> p c e q", e=2),
+                in0=x_tile.rearrange("p (c q e) -> p c e q", q=P, e=2),
+                scalar1=minus_mean[:],
+                scalar2=rstd[:],
+                op0=ALU.add,
+                op1=ALU.mult,
+            )
+
+        def transposes(n):
+            kind, index = preparations[n]
+            if kind == "tokens":
+                banks = [psum.tile([P, BANK], F32, tag="bank", name="bank") for b in range(FEATURE_TILES // 2)]
+                for t in range(GROUP_TILES):
+                    for f in range(FEATURE_TILES):
+                        at = (f % 2) * GROUP + t * P
+                        nc.tensor.transpose(banks[f // 2][:, at : at + P], xn[index * GROUP_TILES + t][:, f, :], ident[:])
+            else:
+                first, rows = chunks[index]
+                words = e_sb[index][:].bitcast(F32)
+                banks = [psum.tile([P, BANK], F32, tag="bank", name="bank") for b in range(rows // P)]
+                for b in range(rows // P):
+                    for w in range(BANK // P):
+                        at = b * BANK + w * P
+                        nc.tensor.transpose(banks[b][:, w * P : (w + 1) * P], words[:, at : at + P], ident[:])
+            banks_of[n] = banks
+
+        def copies_out(n):
+            kind, index = preparations[n]
+            banks = banks_of[n]
+            if kind == "tokens":
+                planes = stage.tile([P, FEATURE_TILES, GROUP], BF16, tag="planes")
+                for f in range(FEATURE_TILES):
+                    c, e = divmod(f, 2)
+                    part = banks[f // 2][:, (f % 2) * GROUP : (f % 2 + 1) * GROUP]
+                    gamma = gain_cols[:, e, c : c + 1]
+                    beta = gain_cols[:, e, 4 + c : 5 + c]
+                    if f // 2 == 0:
+                        nc.vector.tensor_scalar(
+                            out=planes[:, f, :], in0=part, scalar1=gamma, scalar2=beta, op0=ALU.mult, op1=ALU.add
+                        )
+                    else:
+                        nc.scalar.activation(out=planes[:, f, :], in_=part, func=ACT.Identity, bias=beta, scale=gamma)
+                staged[n] = planes
+            else:
+                first, rows = chunks[index]
+                grouped = rows_stage.tile([P, PASSES * CHUNK * PACK], BF16, tag="grouped", align_bytes=64)
+                pairs = grouped[:, : PASSES * rows * PACK].bitcast(F32).rearrange("p (s r u) -> p s r u", s=PASSES, u=2)
+                for b in range(rows // P):
+                    source = banks[b][:].rearrange("p (s u r) -> p s r u", s=PASSES, u=2)
+                    if b == 0:
+                        nc.vector.tensor_copy(out=pairs[:, :, b * P : (b + 1) * P, :], in_=source)
+                    else:
+                        nc.scalar.copy(out=pairs[:, :, b * P : (b + 1) * P, :], in_=source)
+                staged[n] = grouped
+
+        def quantise(n):
+            kind, index = preparations[n]
+            if kind == "tokens":
+                grouped = stage.tile([P, PASSES * GROUP * PACK], BF16, tag="h_grouped", align_bytes=64)
+                nc.vector.tensor_copy(
+                    out=grouped[:].rearrange("p (s r t) -> p s r t", s=PASSES, t=PACK),
+                    in_=staged[n][:].rearrange("p (s t) r -> p s r t", t=PACK),
+                )
+                nc.vector.quantize_mx(out=h_words[index][:].bitcast(FP8X4), scales=h_scales[index][:], in_=grouped[:])
+            else:
+                first, rows = chunks[index]
+                nc.vector.quantize_mx(
+                    out=e_words[index][:].bitcast(FP8X4),
+                    scales=e_scales[index][:],
+                    in_=staged[n][:, : PASSES * rows * PACK],
+                )
+
+        def product(acc, i, c):
+            g, t = divmod(i, GROUP_TILES)
+            first, rows = chunks[c]
+            for s in range(PASSES):
+                tokens = slice(s * GROUP + t * P, s * GROUP + (t + 1) * P)
+                columns = slice(s * rows, (s + 1) * rows)
+                nc.tensor.matmul_mx(
+                    out=acc,
+                    lhsT=h_words[g][:, tokens].bitcast(FP8X4),
+                    lhsT_scale=h_scales[g][:, tokens],
+                    rhs=e_words[c][:, columns].bitcast(FP8X4),
+                    rhs_scale=e_scales[c][:, columns],
+                    start=(s == 0),
+                    stop=(s == PASSES - 1),
+                )
+
+        for i in range(GROUP_TILES):
+            normalise(i)
+        gain_split = keep.tile([P, 2, P], F32, name="gain_split")
+        nc.vector.tensor_copy(out=gain_split[:], in_=gain_rows[:].rearrange("p (q e) -> p e q", e=2))
+        gain_bank = psum.tile([P, BANK], F32, tag="bank")
+        for e in range(2):
+            nc.tensor.transpose(gain_bank[:, e * P : (e + 1) * P], gain_split[:, e, :], ident[:])
+        for i in range(GROUP_TILES, 2 * GROUP_TILES):
+            normalise(i)
+        gain_cols = keep.tile([P, 2, 8], F32, name="gain_cols")
+        nc.vector.tensor_copy(
+            out=gain_cols[:], in_=gain_bank[:, : 2 * P].rearrange("p (e r) -> p e r", e=2)[:, :, 0:8]
+        )
+        for n in range(LOOKAHEAD):
+            transposes(n)
+            copies_out(n)
+            quantise(n)
+
+        unit = 0
+        for half in range(2):
+            for j in range(ROUNDS):
+                for g in range(2 * half, 2 * half + 2):
+                    ahead = unit + LOOKAHEAD
+                    if 1 <= unit <= 2 * GROUP_TILES:
+                        normalise(2 * GROUP_TILES + unit - 1)
+                    if ahead < len(preparations):
+                        transposes(ahead)
+                        copies_out(ahead)
+                    lin_banks = []
+                    gelus = []
+                    for t in range(GROUP_TILES):
+                        i = g * GROUP_TILES + t
+                        pre = psum.tile([P, BANK], F32, tag="bank")
+                        product(pre[:], i, 2 * j)
+                        lin = psum.tile([P, BANK], F32, tag="bank")
+                        product(lin[:], i, 2 * j + 1)
+                        gelu = result.tile([P, CHUNK], F32, tag="gelu")
+                        nc.scalar.activation(out=gelu[:], in_=pre[:], func=ACT.Gelu)
+                        lin_banks.append(lin)
+                        gelus.append(gelu)
+                    if ahead < len(preparations):
+                        quantise(ahead)
+                    for t in range(GROUP_TILES):
+                        i = g * GROUP_TILES + t
+                        gated = result.tile([P, CHUNK], F32, tag="gated")
+                        nc.vector.tensor_tensor(out=gated[:], in0=lin_banks[t][:], in1=gelus[t][:], op=ALU.mult)
+                        nc.sync.dma_start(out=geglu[i * P : (i + 1) * P, j * CHUNK : (j + 1) * CHUNK], in_=gated[:])
+                    unit += 1
+
+        for g in range(GROUPS):
+            acc = psum.tile([P, BANK], F32, tag="bank")
+            for t in range(GROUP_TILES):
+                product(acc[:, t * 2 * QK : (t + 1) * 2 * QK], g * GROUP_TILES + t, QK_CHUNK)
+            qk = result.tile([P, GROUP_TILES, 2 * QK], F32, tag="qk")
+            if g % 2 == 0:
+                nc.scalar.copy(out=qk[:].rearrange("p t c -> p (t c)"), in_=acc[:])
+            else:
+                nc.vector.tensor_copy(out=qk[:].rearrange("p t c -> p (t c)"), in_=acc[:])
+            tokens = slice(g * GROUP, (g + 1) * GROUP)
+            nc.sync.dma_start(out=query[tokens, :].rearrange("(t p) c -> p t c", p=P), in_=qk[:, :, :QK])
+            nc.sync.dma_start(out=key[tokens, :].rearrange("(t p) c -> p t c", p=P), in_=qk[:, :, QK:])

@@ -27,7 +27,8 @@ GROUP_TILES = 2
 GROUP = GROUP_TILES * P
 GROUPS = TOKENS // GROUP
 FEATURE_TILES = D // P
-LOOKAHEAD = 4
+FIRST = 4
+AHEAD = 5
 
 FLOPS = 2 * TOKENS * D * (2 * QK + 2 * EXP)
 
@@ -86,8 +87,9 @@ def tile_latentattentionblock_pa_kernel(tc, x, ln_gamma, ln_beta, expand, out_0,
         load_tokens(0)
         nc.sync.dma_start(out=gain_rows[0:4, :], in_=ln_gamma.rearrange("(r c) -> r c", r=4))
         nc.sync.dma_start(out=gain_rows[4:8, :], in_=ln_beta.rearrange("(r c) -> r c", r=4))
+        load_rows(0)
         load_tokens(1)
-        for c in range(4):
+        for c in range(1, 4):
             load_rows(c)
         load_tokens(2)
         load_tokens(3)
@@ -103,11 +105,12 @@ def tile_latentattentionblock_pa_kernel(tc, x, ln_gamma, ln_beta, expand, out_0,
             keep.tile([P, PASSES * rows], U8, name="e_scales%d" % c, align_bytes=64) for c, (first, rows) in enumerate(chunks)
         ]
 
+        moments = {}
         xn = {}
         banks_of = {}
         staged = {}
 
-        def normalise(i):
+        def statistics(i):
             g, t = divmod(i, GROUP_TILES)
             x_tile = x_sb[g][:, t * D : (t + 1) * D]
             stats = small.tile([P, 2, 6], F32, tag="stats")
@@ -121,17 +124,19 @@ def tile_latentattentionblock_pa_kernel(tc, x, ln_gamma, ln_beta, expand, out_0,
             )
             rstd = small.tile([P, 1], F32, tag="rstd")
             nc.gpsimd.tensor_tensor(out=rstd[:], in0=var_eps[:], in1=minus_half[:], op=ALU.pow)
-            minus_mean = small.tile([P, 1], F32, tag="minus_mean")
-            nc.gpsimd.tensor_scalar(
-                out=minus_mean[:], in0=mean_var[:, 0:1], scalar1=-1.0, scalar2=0.0, op0=ALU.mult, op1=ALU.add
-            )
+            moments[i] = (mean_var, rstd)
+
+        def normalise(i):
+            g, t = divmod(i, GROUP_TILES)
+            x_tile = x_sb[g][:, t * D : (t + 1) * D]
+            mean_var, rstd = moments[i]
             xn[i] = normed.tile([P, FEATURE_TILES, P], F32, tag="xn", name="xn")
-            nc.gpsimd.tensor_scalar(
+            nc.vector.tensor_scalar(
                 out=xn[i][:].rearrange("p (c e) q -> p c e q", e=2),
                 in0=x_tile.rearrange("p (c q e) -> p c e q", q=P, e=2),
-                scalar1=minus_mean[:],
+                scalar1=mean_var[:, 0:1],
                 scalar2=rstd[:],
-                op0=ALU.add,
+                op0=ALU.subtract,
                 op1=ALU.mult,
             )
 
@@ -163,12 +168,7 @@ def tile_latentattentionblock_pa_kernel(tc, x, ln_gamma, ln_beta, expand, out_0,
                     part = banks[f // 2][:, (f % 2) * GROUP : (f % 2 + 1) * GROUP]
                     gamma = gain_cols[:, e, c : c + 1]
                     beta = gain_cols[:, e, 4 + c : 5 + c]
-                    if f // 2 == 0:
-                        nc.vector.tensor_scalar(
-                            out=planes[:, f, :], in0=part, scalar1=gamma, scalar2=beta, op0=ALU.mult, op1=ALU.add
-                        )
-                    else:
-                        nc.scalar.activation(out=planes[:, f, :], in_=part, func=ACT.Identity, bias=beta, scale=gamma)
+                    nc.scalar.activation(out=planes[:, f, :], in_=part, func=ACT.Identity, bias=beta, scale=gamma)
                 staged[n] = planes
             else:
                 first, rows = chunks[index]
@@ -176,10 +176,7 @@ def tile_latentattentionblock_pa_kernel(tc, x, ln_gamma, ln_beta, expand, out_0,
                 pairs = grouped[:, : PASSES * rows * PACK].bitcast(F32).rearrange("p (s r u) -> p s r u", s=PASSES, u=2)
                 for b in range(rows // P):
                     source = banks[b][:].rearrange("p (s u r) -> p s r u", s=PASSES, u=2)
-                    if b == 0:
-                        nc.vector.tensor_copy(out=pairs[:, :, b * P : (b + 1) * P, :], in_=source)
-                    else:
-                        nc.scalar.copy(out=pairs[:, :, b * P : (b + 1) * P, :], in_=source)
+                    nc.scalar.copy(out=pairs[:, :, b * P : (b + 1) * P, :], in_=source)
                 staged[n] = grouped
 
         def quantise(n):
@@ -215,34 +212,37 @@ def tile_latentattentionblock_pa_kernel(tc, x, ln_gamma, ln_beta, expand, out_0,
                     stop=(s == PASSES - 1),
                 )
 
-        for i in range(GROUP_TILES):
-            normalise(i)
+        statistics(0)
         gain_split = keep.tile([P, 2, P], F32, name="gain_split")
         nc.vector.tensor_copy(out=gain_split[:], in_=gain_rows[:].rearrange("p (q e) -> p e q", e=2))
         gain_bank = psum.tile([P, BANK], F32, tag="bank")
         for e in range(2):
             nc.tensor.transpose(gain_bank[:, e * P : (e + 1) * P], gain_split[:, e, :], ident[:])
-        for i in range(GROUP_TILES, 2 * GROUP_TILES):
-            normalise(i)
+        statistics(1)
+        normalise(0)
         gain_cols = keep.tile([P, 2, 8], F32, name="gain_cols")
         nc.vector.tensor_copy(
             out=gain_cols[:], in_=gain_bank[:, : 2 * P].rearrange("p (e r) -> p e r", e=2)[:, :, 0:8]
         )
-        for n in range(LOOKAHEAD):
+        statistics(2)
+        normalise(1)
+        statistics(3)
+        normalise(2)
+        normalise(3)
+        for n in range(FIRST):
             transposes(n)
             copies_out(n)
             quantise(n)
+        started = FIRST
 
         unit = 0
         for half in range(2):
             for j in range(ROUNDS):
                 for g in range(2 * half, 2 * half + 2):
-                    ahead = unit + LOOKAHEAD
+                    if 2 <= unit <= 2 * GROUP_TILES + 1:
+                        normalise(2 * GROUP_TILES + unit - 2)
                     if 1 <= unit <= 2 * GROUP_TILES:
-                        normalise(2 * GROUP_TILES + unit - 1)
-                    if ahead < len(preparations):
-                        transposes(ahead)
-                        copies_out(ahead)
+                        statistics(2 * GROUP_TILES + unit - 1)
                     lin_banks = []
                     gelus = []
                     for t in range(GROUP_TILES):
@@ -255,13 +255,18 @@ def tile_latentattentionblock_pa_kernel(tc, x, ln_gamma, ln_beta, expand, out_0,
                         nc.scalar.activation(out=gelu[:], in_=pre[:], func=ACT.Gelu)
                         lin_banks.append(lin)
                         gelus.append(gelu)
-                    if ahead < len(preparations):
-                        quantise(ahead)
+                    fresh = range(started, min(unit + AHEAD + 1, len(preparations)))
+                    for n in fresh:
+                        transposes(n)
+                        copies_out(n)
                     for t in range(GROUP_TILES):
                         i = g * GROUP_TILES + t
                         gated = result.tile([P, CHUNK], F32, tag="gated")
                         nc.vector.tensor_tensor(out=gated[:], in0=lin_banks[t][:], in1=gelus[t][:], op=ALU.mult)
                         nc.sync.dma_start(out=geglu[i * P : (i + 1) * P, j * CHUNK : (j + 1) * CHUNK], in_=gated[:])
+                    for n in fresh:
+                        quantise(n)
+                        started += 1
                     unit += 1
 
         for g in range(GROUPS):

@@ -28,6 +28,7 @@ GROUP = GROUP_TILES * P
 GROUPS = TOKENS // GROUP
 FEATURE_TILES = D // P
 FIRST = 4
+STORES = 6
 AHEAD = 5
 
 FLOPS = 2 * TOKENS * D * (2 * QK + 2 * EXP)
@@ -67,6 +68,8 @@ def tile_latentattentionblock_pa_kernel(tc, x, ln_gamma, ln_beta, expand, out_0,
         make_identity(nc, ident[:])
         minus_half = keep.tile([P, 1], F32, name="minus_half")
         nc.gpsimd.memset(minus_half[:], -0.5)
+        first_gelu = keep.tile([P, 1], F32, name="first_gelu")
+        nc.scalar.activation(out=first_gelu[:], in_=minus_half[:], func=ACT.Gelu)
 
         x_sb = [keep.tile([P, GROUP_TILES * D], BF16, name="x_sb%d" % g) for g in range(GROUPS)]
         e_sb = [keep.tile([P, (rows // P) * D], BF16, name="e_sb%d" % c) for c, (first, rows) in enumerate(chunks)]
@@ -79,10 +82,11 @@ def tile_latentattentionblock_pa_kernel(tc, x, ln_gamma, ln_beta, expand, out_0,
 
         def load_rows(c):
             first, rows = chunks[c]
-            nc.sync.dma_start(
-                out=e_sb[c][:].rearrange("p (t k) -> p t k", k=D),
-                in_=expand[first : first + rows, :].rearrange("(t p) k -> p t k", p=P),
-            )
+            for h in range(rows // (2 * P)):
+                nc.sync.dma_start(
+                    out=e_sb[c][:, h * 2 * D : (h + 1) * 2 * D].rearrange("p (t k) -> p t k", k=D),
+                    in_=expand[first + h * 2 * P : first + (h + 1) * 2 * P, :].rearrange("(t p) k -> p t k", p=P),
+                )
 
         load_tokens(0)
         nc.sync.dma_start(out=gain_rows[0:4, :], in_=ln_gamma.rearrange("(r c) -> r c", r=4))
@@ -105,17 +109,22 @@ def tile_latentattentionblock_pa_kernel(tc, x, ln_gamma, ln_beta, expand, out_0,
             keep.tile([P, PASSES * rows], U8, name="e_scales%d" % c, align_bytes=64) for c, (first, rows) in enumerate(chunks)
         ]
 
+        halves = {}
         moments = {}
         xn = {}
         banks_of = {}
         staged = {}
 
-        def statistics(i):
+        def sums(i):
             g, t = divmod(i, GROUP_TILES)
             x_tile = x_sb[g][:, t * D : (t + 1) * D]
             stats = small.tile([P, 2, 6], F32, tag="stats")
             for s in range(2):
                 nc.vector.bn_stats(out=stats[:, s, :], in_=x_tile[:, s * 512 : (s + 1) * 512])
+            halves[i] = stats
+
+        def moments_of(i):
+            stats = halves[i]
             mean_var = small.tile([P, 2], F32, tag="mean_var")
             nc.vector.bn_aggr(out=mean_var[:], in_=stats[:].rearrange("p s c -> p (s c)"))
             var_eps = small.tile([P, 1], F32, tag="var_eps")
@@ -212,37 +221,44 @@ def tile_latentattentionblock_pa_kernel(tc, x, ln_gamma, ln_beta, expand, out_0,
                     stop=(s == PASSES - 1),
                 )
 
-        statistics(0)
+        sums(0)
         gain_split = keep.tile([P, 2, P], F32, name="gain_split")
         nc.vector.tensor_copy(out=gain_split[:], in_=gain_rows[:].rearrange("p (q e) -> p e q", e=2))
         gain_bank = psum.tile([P, BANK], F32, tag="bank")
         for e in range(2):
             nc.tensor.transpose(gain_bank[:, e * P : (e + 1) * P], gain_split[:, e, :], ident[:])
-        statistics(1)
-        normalise(0)
+        moments_of(0)
+        sums(1)
         gain_cols = keep.tile([P, 2, 8], F32, name="gain_cols")
         nc.vector.tensor_copy(
             out=gain_cols[:], in_=gain_bank[:, : 2 * P].rearrange("p (e r) -> p e r", e=2)[:, :, 0:8]
         )
-        statistics(2)
+        moments_of(1)
+        normalise(0)
+        sums(2)
         normalise(1)
-        statistics(3)
+        moments_of(2)
+        sums(3)
         normalise(2)
-        normalise(3)
+        moments_of(3)
         for n in range(FIRST):
             transposes(n)
             copies_out(n)
             quantise(n)
+            if n == 0:
+                normalise(3)
         started = FIRST
 
         unit = 0
         for half in range(2):
             for j in range(ROUNDS):
                 for g in range(2 * half, 2 * half + 2):
+                    if 1 <= unit <= 2 * GROUP_TILES:
+                        sums(2 * GROUP_TILES + unit - 1)
                     if 2 <= unit <= 2 * GROUP_TILES + 1:
                         normalise(2 * GROUP_TILES + unit - 2)
                     if 1 <= unit <= 2 * GROUP_TILES:
-                        statistics(2 * GROUP_TILES + unit - 1)
+                        moments_of(2 * GROUP_TILES + unit - 1)
                     lin_banks = []
                     gelus = []
                     for t in range(GROUP_TILES):
@@ -261,7 +277,7 @@ def tile_latentattentionblock_pa_kernel(tc, x, ln_gamma, ln_beta, expand, out_0,
                         copies_out(n)
                     for t in range(GROUP_TILES):
                         i = g * GROUP_TILES + t
-                        gated = result.tile([P, CHUNK], F32, tag="gated")
+                        gated = result.tile([P, CHUNK], F32, tag="gated", bufs=STORES)
                         nc.vector.tensor_tensor(out=gated[:], in0=lin_banks[t][:], in1=gelus[t][:], op=ALU.mult)
                         nc.sync.dma_start(out=geglu[i * P : (i + 1) * P, j * CHUNK : (j + 1) * CHUNK], in_=gated[:])
                     for n in fresh:

from contextlib import ExitStack

import concourse.mybir as mybir
from concourse.masks import make_identity

F32 = mybir.dt.float32
BF16 = mybir.dt.bfloat16
U32 = mybir.dt.uint32
U8 = mybir.dt.uint8
FP8X4 = mybir.dt.float8_e4m3fn_x4
ACT = mybir.ActivationFunctionType
ALU = mybir.AluOpType

P = 128
TOKENS = 1024
D = 1024
QK = 128
EXP = 2048
EPS = 1e-5

PACK = 4
PASSES = D // (P * PACK)
BANK = 512
CHUNK = 512
ROUNDS = EXP // CHUNK
GROUP_TILES = 2
GROUP = GROUP_TILES * P
GROUPS = TOKENS // GROUP
FEATURE_TILES = D // P
FIRST = 4
STORES = 6
AHEAD = 5

FLOPS = 2 * TOKENS * D * (2 * QK + 2 * EXP)


def tile_latentattentionblock_pa_kernel(tc, x, ln_gamma, ln_beta, expand, out_0, out_1, out_2):
    nc = tc.nc
    x_rows = x.flatten_outer_dims()
    query = out_0.flatten_outer_dims()
    key = out_1.flatten_outer_dims()
    geglu = out_2.flatten_outer_dims()

    chunks = []
    for j in range(ROUNDS):
        chunks.append((2 * QK + EXP + j * CHUNK, CHUNK))
        chunks.append((2 * QK + j * CHUNK, CHUNK))
    QK_CHUNK = len(chunks)
    chunks.append((0, 2 * QK))

    preparations = [("rows", 0), ("tokens", 0), ("rows", 1), ("tokens", 1)]
    preparations.extend([("rows", c) for c in range(2, QK_CHUNK)])
    preparations.extend([("tokens", 2), ("tokens", 3), ("rows", QK_CHUNK)])

    with ExitStack() as ctx:
        keep = ctx.enter_context(tc.tile_pool(name="keep", bufs=1))
        small = ctx.enter_context(tc.tile_pool(name="small", bufs=4))
        normed = ctx.enter_context(tc.tile_pool(name="normed", bufs=2 * GROUP_TILES))
        stage = ctx.enter_context(tc.tile_pool(name="stage", bufs=2))
        rows_stage = ctx.enter_context(tc.tile_pool(name="rows_stage", bufs=3))
        result = ctx.enter_context(tc.tile_pool(name="result", bufs=4))
        psum = ctx.enter_context(tc.psum_pool(name="psum", bufs=8))
        ctx.enter_context(tc.manual_schedule())

        gain_rows = keep.tile([P, 2 * P], BF16, name="gain_rows")
        nc.gpsimd.memset(gain_rows[:], 0.0)
        ident = keep.tile([P, P], F32, name="ident")
        make_identity(nc, ident[:])
        minus_half = keep.tile([P, 1], F32, name="minus_half")
        nc.gpsimd.memset(minus_half[:], -0.5)
        first_gelu = keep.tile([P, 1], F32, name="first_gelu")
        nc.scalar.activation(out=first_gelu[:], in_=minus_half[:], func=ACT.Gelu)

        x_sb = [keep.tile([P, GROUP_TILES * D], BF16, name="x_sb%d" % g) for g in range(GROUPS)]
        e_sb = [keep.tile([P, (rows // P) * D], BF16, name="e_sb%d" % c) for c, (first, rows) in enumerate(chunks)]

        def load_tokens(g):
            nc.sync.dma_start(
                out=x_sb[g][:].rearrange("p (t k) -> p t k", k=D),
                in_=x_rows[g * GROUP : (g + 1) * GROUP, :].rearrange("(t p) k -> p t k", p=P),
            )

        def load_rows(c):
            first, rows = chunks[c]
            for h in range(rows // (2 * P)):
                nc.sync.dma_start(
                    out=e_sb[c][:, h * 2 * D : (h + 1) * 2 * D].rearrange("p (t k) -> p t k", k=D),
                    in_=expand[first + h * 2 * P : first + (h + 1) * 2 * P, :].rearrange("(t p) k -> p t k", p=P),
                )

        load_tokens(0)
        nc.sync.dma_start(out=gain_rows[0:4, :], in_=ln_gamma.rearrange("(r c) -> r c", r=4))
        nc.sync.dma_start(out=gain_rows[4:8, :], in_=ln_beta.rearrange("(r c) -> r c", r=4))
        load_rows(0)
        load_tokens(1)
        for c in range(1, 4):
            load_rows(c)
        load_tokens(2)
        load_tokens(3)
        for c in range(4, len(chunks)):
            load_rows(c)

        h_words = [keep.tile([P, PASSES * GROUP], U32, name="h_words%d" % g, align_bytes=64) for g in range(GROUPS)]
        h_scales = [keep.tile([P, PASSES * GROUP], U8, name="h_scales%d" % g, align_bytes=64) for g in range(GROUPS)]
        e_words = [
            keep.tile([P, PASSES * rows], U32, name="e_words%d" % c, align_bytes=64) for c, (first, rows) in enumerate(chunks)
        ]
        e_scales = [
            keep.tile([P, PASSES * rows], U8, name="e_scales%d" % c, align_bytes=64) for c, (first, rows) in enumerate(chunks)
        ]

        halves = {}
        moments = {}
        xn = {}
        banks_of = {}
        staged = {}

        def sums(i):
            g, t = divmod(i, GROUP_TILES)
            x_tile = x_sb[g][:, t * D : (t + 1) * D]
            stats = small.tile([P, 2, 6], F32, tag="stats")
            for s in range(2):
                nc.vector.bn_stats(out=stats[:, s, :], in_=x_tile[:, s * 512 : (s + 1) * 512])
            halves[i] = stats

        def moments_of(i):
            stats = halves[i]
            mean_var = small.tile([P, 2], F32, tag="mean_var")
            nc.vector.bn_aggr(out=mean_var[:], in_=stats[:].rearrange("p s c -> p (s c)"))
            var_eps = small.tile([P, 1], F32, tag="var_eps")
            nc.gpsimd.tensor_scalar(
                out=var_eps[:], in0=mean_var[:, 1:2], scalar1=EPS, scalar2=1.0, op0=ALU.add, op1=ALU.mult
            )
            rstd = small.tile([P, 1], F32, tag="rstd")
            nc.gpsimd.tensor_tensor(out=rstd[:], in0=var_eps[:], in1=minus_half[:], op=ALU.pow)
            moments[i] = (mean_var, rstd)

        def normalise(i):
            g, t = divmod(i, GROUP_TILES)
            x_tile = x_sb[g][:, t * D : (t + 1) * D]
            mean_var, rstd = moments[i]
            xn[i] = normed.tile([P, FEATURE_TILES, P], F32, tag="xn", name="xn")
            nc.vector.tensor_scalar(
                out=xn[i][:].rearrange("p (c e) q -> p c e q", e=2),
                in0=x_tile.rearrange("p (c q e) -> p c e q", q=P, e=2),
                scalar1=mean_var[:, 0:1],
                scalar2=rstd[:],
                op0=ALU.subtract,
                op1=ALU.mult,
            )

        def transposes(n):
            kind, index = preparations[n]
            if kind == "tokens":
                banks = [psum.tile([P, BANK], F32, tag="bank", name="bank") for b in range(FEATURE_TILES // 2)]
                for t in range(GROUP_TILES):
                    for f in range(FEATURE_TILES):
                        at = (f % 2) * GROUP + t * P
                        nc.tensor.transpose(banks[f // 2][:, at : at + P], xn[index * GROUP_TILES + t][:, f, :], ident[:])
            else:
                first, rows = chunks[index]
                words = e_sb[index][:].bitcast(F32)
                banks = [psum.tile([P, BANK], F32, tag="bank", name="bank") for b in range(rows // P)]
                for b in range(rows // P):
                    for w in range(BANK // P):
                        at = b * BANK + w * P
                        nc.tensor.transpose(banks[b][:, w * P : (w + 1) * P], words[:, at : at + P], ident[:])
            banks_of[n] = banks

        def copies_out(n):
            kind, index = preparations[n]
            banks = banks_of[n]
            if kind == "tokens":
                planes = stage.tile([P, FEATURE_TILES, GROUP], BF16, tag="planes")
                for f in range(FEATURE_TILES):
                    c, e = divmod(f, 2)
                    part = banks[f // 2][:, (f % 2) * GROUP : (f % 2 + 1) * GROUP]
                    gamma = gain_cols[:, e, c : c + 1]
                    beta = gain_cols[:, e, 4 + c : 5 + c]
                    nc.scalar.activation(out=planes[:, f, :], in_=part, func=ACT.Identity, bias=beta, scale=gamma)
                staged[n] = planes
            else:
                first, rows = chunks[index]
                grouped = rows_stage.tile([P, PASSES * CHUNK * PACK], BF16, tag="grouped", align_bytes=64)
                pairs = grouped[:, : PASSES * rows * PACK].bitcast(F32).rearrange("p (s r u) -> p s r u", s=PASSES, u=2)
                for b in range(rows // P):
                    source = banks[b][:].rearrange("p (s u r) -> p s r u", s=PASSES, u=2)
                    nc.scalar.copy(out=pairs[:, :, b * P : (b + 1) * P, :], in_=source)
                staged[n] = grouped

        def quantise(n):
            kind, index = preparations[n]
            if kind == "tokens":
                grouped = stage.tile([P, PASSES * GROUP * PACK], BF16, tag="h_grouped", align_bytes=64)
                nc.vector.tensor_copy(
                    out=grouped[:].rearrange("p (s r t) -> p s r t", s=PASSES, t=PACK),
                    in_=staged[n][:].rearrange("p (s t) r -> p s r t", t=PACK),
                )
                nc.vector.quantize_mx(out=h_words[index][:].bitcast(FP8X4), scales=h_scales[index][:], in_=grouped[:])
            else:
                first, rows = chunks[index]
                nc.vector.quantize_mx(
                    out=e_words[index][:].bitcast(FP8X4),
                    scales=e_scales[index][:],
                    in_=staged[n][:, : PASSES * rows * PACK],
                )

        def product(acc, i, c):
            g, t = divmod(i, GROUP_TILES)
            first, rows = chunks[c]
            for s in range(PASSES):
                tokens = slice(s * GROUP + t * P, s * GROUP + (t + 1) * P)
                columns = slice(s * rows, (s + 1) * rows)
                nc.tensor.matmul_mx(
                    out=acc,
                    lhsT=h_words[g][:, tokens].bitcast(FP8X4),
                    lhsT_scale=h_scales[g][:, tokens],
                    rhs=e_words[c][:, columns].bitcast(FP8X4),
                    rhs_scale=e_scales[c][:, columns],
                    start=(s == 0),
                    stop=(s == PASSES - 1),
                )

        sums(0)
        gain_split = keep.tile([P, 2, P], F32, name="gain_split")
        nc.vector.tensor_copy(out=gain_split[:], in_=gain_rows[:].rearrange("p (q e) -> p e q", e=2))
        gain_bank = psum.tile([P, BANK], F32, tag="bank")
        for e in range(2):
            nc.tensor.transpose(gain_bank[:, e * P : (e + 1) * P], gain_split[:, e, :], ident[:])
        moments_of(0)
        sums(1)
        gain_cols = keep.tile([P, 2, 8], F32, name="gain_cols")
        nc.vector.tensor_copy(
            out=gain_cols[:], in_=gain_bank[:, : 2 * P].rearrange("p (e r) -> p e r", e=2)[:, :, 0:8]
        )
        moments_of(1)
        normalise(0)
        sums(2)
        normalise(1)
        moments_of(2)
        sums(3)
        normalise(2)
        moments_of(3)
        for n in range(FIRST):
            transposes(n)
            copies_out(n)
            quantise(n)
            if n == 0:
                normalise(3)
        started = FIRST

        unit = 0
        for half in range(2):
            for j in range(ROUNDS):
                for g in range(2 * half, 2 * half + 2):
                    if 1 <= unit <= 2 * GROUP_TILES:
                        sums(2 * GROUP_TILES + unit - 1)
                    if 2 <= unit <= 2 * GROUP_TILES + 1:
                        normalise(2 * GROUP_TILES + unit - 2)
                    if 1 <= unit <= 2 * GROUP_TILES:
                        moments_of(2 * GROUP_TILES + unit - 1)
                    lin_banks = []
                    gelus = []
                    for t in range(GROUP_TILES):
                        i = g * GROUP_TILES + t
                        pre = psum.tile([P, BANK], F32, tag="bank")
                        product(pre[:], i, 2 * j)
                        lin = psum.tile([P, BANK], F32, tag="bank")
                        product(lin[:], i, 2 * j + 1)
                        gelu = result.tile([P, CHUNK], F32, tag="gelu")
                        nc.scalar.activation(out=gelu[:], in_=pre[:], func=ACT.Gelu)
                        lin_banks.append(lin)
                        gelus.append(gelu)
                    fresh = range(started, min(unit + AHEAD + 1, len(preparations)))
                    for n in fresh:
                        transposes(n)
                        copies_out(n)
                    for t in range(GROUP_TILES):
                        i = g * GROUP_TILES + t
                        gated = result.tile([P, CHUNK], F32, tag="gated", bufs=STORES)
                        nc.vector.tensor_tensor(out=gated[:], in0=lin_banks[t][:], in1=gelus[t][:], op=ALU.mult)
                        nc.sync.dma_start(out=geglu[i * P : (i + 1) * P, j * CHUNK : (j + 1) * CHUNK], in_=gated[:])
                    for n in fresh:
                        quantise(n)
                        started += 1
                    unit += 1

        for g in range(GROUPS):
            acc = psum.tile([P, BANK], F32, tag="bank")
            for t in range(GROUP_TILES):
                product(acc[:, t * 2 * QK : (t + 1) * 2 * QK], g * GROUP_TILES + t, QK_CHUNK)
            qk = result.tile([P, GROUP_TILES, 2 * QK], F32, tag="qk")
            if g % 2 == 0:
                nc.scalar.copy(out=qk[:].rearrange("p t c -> p (t c)"), in_=acc[:])
            else:
                nc.vector.tensor_copy(out=qk[:].rearrange("p t c -> p (t c)"), in_=acc[:])
            tokens = slice(g * GROUP, (g + 1) * GROUP)
            nc.sync.dma_start(out=query[tokens, :].rearrange("(t p) c -> p t c", p=P), in_=qk[:, :, :QK])
            nc.sync.dma_start(out=key[tokens, :].rearrange("(t p) c -> p t c", p=P), in_=qk[:, :, QK:])
